import numpy as np
import ml_dtypes


def mxq(x, axis, fmt="e4m3"):
    dtype, down = {"e4m3": (ml_dtypes.float8_e4m3fn, 7), "e5m2": (ml_dtypes.float8_e5m2, 14)}[fmt]
    v = np.moveaxis(np.asarray(x, np.float32).astype(ml_dtypes.bfloat16).astype(np.float64), axis, -1)
    blocks = v.reshape(v.shape[:-1] + (-1, 32))
    amax = np.abs(blocks).max(-1, keepdims=True)
    byte = np.maximum(np.where(amax > 0, np.frexp(amax)[1] - 1 + 127, 0) - down, 1)
    scale = np.exp2(byte - 127.0)
    codes = (blocks / scale).astype(np.float32).astype(dtype).astype(np.float64)
    return np.moveaxis((codes * scale).reshape(v.shape), -1, axis)


WIDE = False


def mx_kscale(k):
    if not WIDE:
        return np.ones(k)
    levels = np.array([10, -10, 5, -5, 0])
    a = np.random.permutation(np.resize(levels, k // 512 * 4)).reshape(k // 512, 4)
    idx = np.arange(k)
    return np.exp2(a[idx // 512, idx % 128 // 32])


BF16 = ml_dtypes.bfloat16


def bf(x):
    return np.asarray(x, np.float32).astype(BF16)


def f64(x):
    return np.asarray(x).astype(np.float64)


B, C, H, WI, D, N = 128, 1, 32, 32, 512, 1024
F = C * H * WI
MARGIN, SCALE = 50.0, 5.0
TARGET = 51.5
LN = np.log(N)
ZN = np.sqrt(2.0 * LN) - (np.log(LN) + np.log(4.0 * np.pi)) / (2.0 * np.sqrt(2.0 * LN))
SIG = TARGET / np.sqrt(2.0 * D - ZN * np.sqrt(6.0 * D))


def setup_inputs():
    s = mx_kscale(F)
    x = bf((np.random.standard_normal((B, F)) * s).reshape(B, C, H, WI))
    y = bf(f64(x) + 1.4 * np.random.standard_normal((B, C, H, WI)))
    W = bf(np.random.standard_normal((F, D)) * SIG / np.sqrt(F) / s[:, None])
    lookup = bf(np.random.standard_normal((N, D)) * SIG)
    return {"x": x, "y": y, "W": W, "lookup": lookup}


def reference(x, y, W, lookup):
    x, y, W, lookup = f64(x), f64(y), f64(W), f64(lookup)
    nb = x.shape[0]
    emb = mxq(x.reshape(nb, -1), 1, "e4m3") @ mxq(W, 0, "e4m3")
    sq = (
        np.sum(emb * emb, axis=-1)[:, None]
        + np.sum(lookup * lookup, axis=-1)[None, :]
        - 2.0 * (mxq(emb, 1, "e4m3") @ mxq(lookup, 1, "e4m3").T)
    )
    dist = np.sqrt(np.maximum(sq, 0.0))
    min_d = np.min(dist, axis=1)
    mse = np.mean((x - y) ** 2)
    return mse + np.minimum(MARGIN - min_d, 0.0) * SCALE

@@ -1,0 +1,238 @@
+from contextlib import ExitStack
+
+import concourse.mybir as mybir
+from concourse.masks import make_identity
+
+F32 = mybir.dt.float32
+BF16 = mybir.dt.bfloat16
+U32 = mybir.dt.uint32
+U8 = mybir.dt.uint8
+FP8X4 = mybir.dt.float8_e4m3fn_x4
+ACT = mybir.ActivationFunctionType
+ALU = mybir.AluOpType
+
+P = 128
+PACK = 4
+K_PASS = P * PACK
+
+BATCH = 128
+PIXELS = 1024
+DIM = 512
+ROWS = 1024
+MARGIN = 50.0
+SCALE = 5.0
+
+PASSES = PIXELS // K_PASS
+BLOCKS = ROWS // P
+PIECES = 4
+PER_PIECE = BLOCKS // PIECES
+CHAINS = 2
+BANK = 512
+
+FLOPS = 2 * BATCH * PIXELS * DIM + 2 * BATCH * DIM * ROWS
+
+
+def tile_privacyloss_s_kernel(tc, x, y, W, lookup, out):
+    nc = tc.nc
+    with ExitStack() as ctx:
+        keep = ctx.enter_context(tc.tile_pool(name="keep", bufs=1))
+        psum_plain = ctx.enter_context(tc.psum_pool(name="psum_plain", bufs=4))
+        psum_mx = ctx.enter_context(tc.psum_pool(name="psum_mx", bufs=1))
+
+        ident = keep.tile([P, P], F32)
+        make_identity(nc, ident[:])
+        mean_weight = keep.tile([P, P], F32)
+        nc.gpsimd.memset(mean_weight[:], 1.0 / (BATCH * PIXELS))
+        neg_margin = keep.tile([P, 1], F32)
+        nc.vector.memset(neg_margin[:], -MARGIN * SCALE)
+        warm = keep.tile([P, 1], F32)
+        nc.vector.memset(warm[:], 1.0)
+        nc.scalar.activation(out=warm[:], in_=warm[:], func=ACT.Sqrt)
+
+        x_sb = keep.tile([P, PIXELS], BF16)
+        nc.sync.dma_start(out=x_sb[:], in_=x.rearrange("b c h w -> b (c h w)"))
+        w_rows = W.rearrange("(g u p e) d -> g p u (e d)", g=PASSES, u=2, e=2)
+        w_raw = []
+        for g in range(PASSES):
+            w_raw.append(keep.tile([P, PACK, DIM], BF16, name="w_raw%d" % g))
+            nc.sync.dma_start(
+                out=w_raw[g][:].rearrange("p (u e) d -> p u (e d)", u=2), in_=w_rows[g]
+            )
+        lookup_rows = lookup.rearrange("(p c) d -> p c d", c=BLOCKS)
+        lk = []
+        for j in range(PIECES):
+            lk.append(keep.tile([P, PER_PIECE, DIM], BF16, name="lk%d" % j))
+            nc.sync.dma_start(
+                out=lk[j][:], in_=lookup_rows[:, PER_PIECE * j : PER_PIECE * (j + 1), :]
+            )
+        y_sb = keep.tile([P, PIXELS], BF16)
+        nc.sync.dma_start(out=y_sb[:], in_=y.rearrange("b c h w -> b (c h w)"))
+
+        x_words = x_sb[:].bitcast(F32)
+        x_t = psum_plain.tile([P, BANK], F32, tag="plain")
+        for gu in range(PASSES * 2):
+            cols = slice(P * gu, P * (gu + 1))
+            nc.tensor.transpose(x_t[:, cols], x_words[:, cols], ident[:])
+        x_grouped = keep.tile([P, PASSES * BATCH * PACK], BF16, align_bytes=64)
+        nc.scalar.copy(
+            out=x_grouped[:].bitcast(F32).rearrange("p (g b u) -> p g b u", g=PASSES, u=2),
+            in_=x_t[:].rearrange("p (g u b) -> p g b u", g=PASSES, u=2),
+        )
+        x_codes = keep.tile([P, PASSES, BATCH], U32, align_bytes=64)
+        x_scales = keep.tile([P, PASSES, BATCH], U8, align_bytes=64)
+
+        w_grouped = []
+        w_codes = []
+        w_scales = []
+        for g in range(PASSES):
+            w_grouped.append(keep.tile([P, DIM * PACK], BF16, name="w_grouped%d" % g, align_bytes=64))
+            w_codes.append(keep.tile([P, DIM], U32, name="w_codes%d" % g, align_bytes=64))
+            w_scales.append(keep.tile([P, DIM], U8, name="w_scales%d" % g, align_bytes=64))
+            nc.vector.tensor_copy(
+                out=w_grouped[g][:].rearrange("p (h f i t) -> p h f i t", h=2, f=2, t=PACK),
+                in_=w_raw[g][:].rearrange("p t (h i f) -> p h f i t", h=2, f=2),
+            )
+            if g == 0:
+                nc.vector.quantize_mx(
+                    out=x_codes[:].rearrange("p g b -> p (g b)").bitcast(FP8X4),
+                    scales=x_scales[:].rearrange("p g b -> p (g b)"),
+                    in_=x_grouped[:],
+                )
+        for g in range(PASSES):
+            nc.vector.quantize_mx(
+                out=w_codes[g][:].bitcast(FP8X4), scales=w_scales[g][:], in_=w_grouped[g][:]
+            )
+
+        emb_t = psum_mx.tile([P, PACK, BATCH], F32)
+        for t in range(PACK):
+            for g in range(PASSES):
+                nc.tensor.matmul_mx(
+                    out=emb_t[:, t, :],
+                    lhsT=w_codes[g][:, P * t : P * (t + 1)].bitcast(FP8X4),
+                    lhsT_scale=w_scales[g][:, P * t : P * (t + 1)],
+                    rhs=x_codes[:, g, :].bitcast(FP8X4),
+                    rhs_scale=x_scales[:, g, :],
+                    start=(g == 0),
+                    stop=(g == PASSES - 1),
+                )
+        emb = psum_mx.tile([P, DIM], F32)
+        for g in range(PASSES):
+            nc.tensor.matmul_mx(
+                out=emb[:],
+                lhsT=x_codes[:, g, :].bitcast(FP8X4),
+                lhsT_scale=x_scales[:, g, :],
+                rhs=w_codes[g][:].bitcast(FP8X4),
+                rhs_scale=w_scales[g][:],
+                start=(g == 0),
+                stop=(g == PASSES - 1),
+            )
+        emb_grouped = keep.tile([P, BATCH, PACK], BF16, align_bytes=64)
+        nc.vector.tensor_copy(out=emb_grouped[:], in_=emb_t[:].rearrange("p t b -> p b t"))
+        emb_squares = keep.tile([P, DIM], F32)
+        emb_norm = keep.tile([P, 1], F32)
+        nc.scalar.activation(out=emb_squares[:], in_=emb[:], func=ACT.Square, accum_out=emb_norm[:])
+
+        lk_norm = keep.tile([P, BLOCKS], F32)
+        lk_squares = keep.tile([P, DIM], BF16)
+        lk_codes = []
+        lk_scales = []
+        for j in range(PIECES):
+            for c in range(PER_PIECE):
+                block = PER_PIECE * j + c
+                nc.scalar.activation(
+                    out=lk_squares[:],
+                    in_=lk[j][:, c, :],
+                    func=ACT.Square,
+                    accum_out=lk_norm[:, block : block + 1],
+                )
+            lk_words = lk[j][:].rearrange("p c d -> p (c d)").bitcast(F32)
+            lk_t = psum_plain.tile([P, BANK], F32, tag="plain")
+            for cu in range(PER_PIECE * 2):
+                cols = slice(P * cu, P * (cu + 1))
+                nc.tensor.transpose(lk_t[:, cols], lk_words[:, cols], ident[:])
+            lk_grouped = keep.tile([P, PER_PIECE * P * PACK], BF16, name="lk_grouped%d" % j, align_bytes=64)
+            grouped_words = lk_grouped[:].bitcast(F32).rearrange("p (c n u) -> p c n u", c=PER_PIECE, u=2)
+            transposed_words = lk_t[:].rearrange("p (c u n) -> p c n u", c=PER_PIECE, u=2)
+            if j % 2 == 0:
+                nc.vector.tensor_copy(out=grouped_words, in_=transposed_words)
+            else:
+                nc.scalar.copy(out=grouped_words, in_=transposed_words)
+            lk_codes.append(keep.tile([P, PER_PIECE, P], U32, name="lk_codes%d" % j, align_bytes=64))
+            lk_scales.append(keep.tile([P, PER_PIECE, P], U8, name="lk_scales%d" % j, align_bytes=64))
+            nc.vector.quantize_mx(
+                out=lk_codes[j][:].rearrange("p c n -> p (c n)").bitcast(FP8X4),
+                scales=lk_scales[j][:].rearrange("p c n -> p (c n)"),
+                in_=lk_grouped[:],
+            )
+        lk_half_norm = keep.tile([P, BLOCKS], F32)
+        nc.scalar.mul(out=lk_half_norm[:], in_=lk_norm[:], mul=0.5)
+
+        emb_codes = keep.tile([P, BATCH], U32, align_bytes=64)
+        emb_scales = keep.tile([P, BATCH], U8, align_bytes=64)
+        nc.vector.quantize_mx(
+            out=emb_codes[:].bitcast(FP8X4),
+            scales=emb_scales[:],
+            in_=emb_grouped[:].rearrange("p b t -> p (b t)"),
+        )
+
+        diff = keep.tile([P, PIXELS], F32)
+        nc.vector.tensor_tensor(out=diff[:], in0=x_sb[:], in1=y_sb[:], op=ALU.subtract)
+        diff_norm = keep.tile([P, 1], F32)
+        nc.scalar.activation(out=diff[:], in_=diff[:], func=ACT.Square, accum_out=diff_norm[:])
+
+        per_bank = BANK // BATCH
+        dots = []
+        for half in range(BLOCKS // per_bank):
+            dots.append(psum_mx.tile([P, per_bank, BATCH], F32, name="dots%d" % half))
+        for block in range(BLOCKS):
+            nc.tensor.matmul_mx(
+                out=dots[block // per_bank][:, block % per_bank, :],
+                lhsT=lk_codes[block // PER_PIECE][:, block % PER_PIECE, :].bitcast(FP8X4),
+                lhsT_scale=lk_scales[block // PER_PIECE][:, block % PER_PIECE, :],
+                rhs=emb_codes[:].bitcast(FP8X4),
+                rhs_scale=emb_scales[:],
+                start=True,
+                stop=True,
+            )
+        best = keep.tile([P, CHAINS, BATCH], F32)
+        for block in range(BLOCKS):
+            running = best[:, block % CHAINS, :]
+            scores = dots[block // per_bank][:, block % per_bank, :]
+            half_norm = lk_half_norm[:, block : block + 1]
+            if block < CHAINS:
+                nc.vector.tensor_scalar(
+                    out=running, in0=scores, scalar1=half_norm, scalar2=None, op0=ALU.subtract
+                )
+            else:
+                nc.vector.scalar_tensor_tensor(
+                    out=running, in0=scores, scalar=half_norm, in1=running,
+                    op0=ALU.subtract, op1=ALU.max,
+                )
+
+        mse_ps = psum_plain.tile([P, BANK], F32, tag="plain")
+        nc.tensor.matmul(out=mse_ps[:, 0:1], lhsT=mean_weight[:], rhs=diff_norm[:], start=True, stop=True)
+        mse = keep.tile([P, 1], F32)
+        nc.scalar.copy(out=mse[:], in_=mse_ps[:, 0:1])
+
+        best_t = psum_plain.tile([P, BANK], F32, tag="plain")
+        for chain in range(CHAINS):
+            nc.tensor.transpose(best_t[:, P * chain : P * (chain + 1)], best[:, chain, :], ident[:])
+        top = keep.tile([P, 1], F32)
+        nc.vector.tensor_reduce(
+            out=top[:], in_=best_t[:, 0 : P * CHAINS], axis=mybir.AxisListType.X, op=ALU.max
+        )
+        sq_min = keep.tile([P, 1], F32)
+        nc.scalar.activation(out=sq_min[:], in_=top[:], func=ACT.Relu, scale=-2.0, bias=emb_norm[:])
+        scaled_dist = keep.tile([P, 1], F32)
+        nc.scalar.activation(out=scaled_dist[:], in_=sq_min[:], func=ACT.Sqrt, scale=SCALE * SCALE)
+        excess = keep.tile([P, 1], F32)
+        nc.scalar.activation(out=excess[:], in_=scaled_dist[:], func=ACT.Relu, bias=neg_margin[:])
+
+        excess_row = psum_plain.tile([P, BANK], F32, tag="plain")
+        nc.tensor.transpose(excess_row[:, 0:P], excess[:].to_broadcast([P, P]), ident[:])
+        result = keep.tile([P, BATCH], F32)
+        nc.vector.tensor_scalar(
+            out=result[:], in0=excess_row[:, 0:P], scalar1=-1.0, scalar2=mse[:],
+            op0=ALU.mult, op1=ALU.add,
+        )
+        nc.sync.dma_start(out=out.rearrange("(o b) -> o b", o=1), in_=result[0:1, :])

@@ -1,3 +1,4 @@
+import math
 from contextlib import ExitStack
 
 import concourse.mybir as mybir
@@ -26,6 +27,8 @@ PASSES = PIXELS // K_PASS
 BLOCKS = ROWS // P
 PIECES = 4
 PER_PIECE = BLOCKS // PIECES
+SCALAR_PIECES = 3
+READY_PIECES = 2
 CHAINS = 2
 BANK = 512
 
@@ -38,6 +41,7 @@ def tile_privacyloss_s_kernel(tc, x, y, W, lookup, out):
         keep = ctx.enter_context(tc.tile_pool(name="keep", bufs=1))
         psum_plain = ctx.enter_context(tc.psum_pool(name="psum_plain", bufs=4))
         psum_mx = ctx.enter_context(tc.psum_pool(name="psum_mx", bufs=1))
+        ctx.enter_context(tc.manual_schedule())
 
         ident = keep.tile([P, P], F32)
         make_identity(nc, ident[:])
@@ -50,22 +54,29 @@ def tile_privacyloss_s_kernel(tc, x, y, W, lookup, out):
         nc.scalar.activation(out=warm[:], in_=warm[:], func=ACT.Sqrt)
 
         x_sb = keep.tile([P, PIXELS], BF16)
-        nc.sync.dma_start(out=x_sb[:], in_=x.rearrange("b c h w -> b (c h w)"))
-        w_rows = W.rearrange("(g u p e) d -> g p u (e d)", g=PASSES, u=2, e=2)
+        y_sb = keep.tile([P, PIXELS], BF16)
         w_raw = []
         for g in range(PASSES):
             w_raw.append(keep.tile([P, PACK, DIM], BF16, name="w_raw%d" % g))
-            nc.sync.dma_start(
-                out=w_raw[g][:].rearrange("p (u e) d -> p u (e d)", u=2), in_=w_rows[g]
-            )
-        lookup_rows = lookup.rearrange("(p c) d -> p c d", c=BLOCKS)
         lk = []
         for j in range(PIECES):
             lk.append(keep.tile([P, PER_PIECE, DIM], BF16, name="lk%d" % j))
+        w_rows = W.rearrange("(g u p e) d -> g p u (e d)", g=PASSES, u=2, e=2)
+        lookup_rows = lookup.rearrange("(p c) d -> p c d", c=BLOCKS)
+
+        def load_lookup(j):
             nc.sync.dma_start(
                 out=lk[j][:], in_=lookup_rows[:, PER_PIECE * j : PER_PIECE * (j + 1), :]
             )
-        y_sb = keep.tile([P, PIXELS], BF16)
+
+        nc.sync.dma_start(out=x_sb[:], in_=x.rearrange("b c h w -> b (c h w)"))
+        for g in range(PASSES):
+            nc.sync.dma_start(
+                out=w_raw[g][:].rearrange("p (u e) d -> p u (e d)", u=2), in_=w_rows[g]
+            )
+            load_lookup(g)
+        for j in range(PASSES, PIECES):
+            load_lookup(j)
         nc.sync.dma_start(out=y_sb[:], in_=y.rearrange("b c h w -> b (c h w)"))
 
         x_words = x_sb[:].bitcast(F32)
@@ -88,20 +99,72 @@ def tile_privacyloss_s_kernel(tc, x, y, W, lookup, out):
             w_grouped.append(keep.tile([P, DIM * PACK], BF16, name="w_grouped%d" % g, align_bytes=64))
             w_codes.append(keep.tile([P, DIM], U32, name="w_codes%d" % g, align_bytes=64))
             w_scales.append(keep.tile([P, DIM], U8, name="w_scales%d" % g, align_bytes=64))
-            nc.vector.tensor_copy(
-                out=w_grouped[g][:].rearrange("p (h f i t) -> p h f i t", h=2, f=2, t=PACK),
-                in_=w_raw[g][:].rearrange("p t (h i f) -> p h f i t", h=2, f=2),
-            )
-            if g == 0:
-                nc.vector.quantize_mx(
-                    out=x_codes[:].rearrange("p g b -> p (g b)").bitcast(FP8X4),
-                    scales=x_scales[:].rearrange("p g b -> p (g b)"),
-                    in_=x_grouped[:],
-                )
+        nc.vector.tensor_copy(
+            out=w_grouped[0][:].rearrange("p (h f i t) -> p h f i t", h=2, f=2, t=PACK),
+            in_=w_raw[0][:].rearrange("p t (h i f) -> p h f i t", h=2, f=2),
+        )
+        nc.vector.quantize_mx(
+            out=x_codes[:].rearrange("p g b -> p (g b)").bitcast(FP8X4),
+            scales=x_scales[:].rearrange("p g b -> p (g b)"),
+            in_=x_grouped[:],
+        )
+        nc.vector.tensor_copy(
+            out=w_grouped[1][:].rearrange("p (h f i t) -> p h f i t", h=2, f=2, t=PACK),
+            in_=w_raw[1][:].rearrange("p t (h i f) -> p h f i t", h=2, f=2),
+        )
         for g in range(PASSES):
             nc.vector.quantize_mx(
                 out=w_codes[g][:].bitcast(FP8X4), scales=w_scales[g][:], in_=w_grouped[g][:]
             )
+
+        diff = keep.tile([P, PIXELS], F32)
+        nc.gpsimd.tensor_tensor(out=diff[:], in0=x_sb[:], in1=y_sb[:], op=ALU.subtract)
+
+        lk_half_norm = keep.tile([P, BLOCKS], F32)
+        lk_squares = keep.tile([P, DIM], BF16)
+        lk_t = []
+        lk_grouped = []
+        lk_codes = []
+        lk_scales = []
+        for j in range(PIECES):
+            lk_grouped.append(keep.tile([P, PER_PIECE * P * PACK], BF16, name="lk_grouped%d" % j, align_bytes=64))
+            lk_codes.append(keep.tile([P, PER_PIECE, P], U32, name="lk_codes%d" % j, align_bytes=64))
+            lk_scales.append(keep.tile([P, PER_PIECE, P], U8, name="lk_scales%d" % j, align_bytes=64))
+
+        def half_norm_of(block):
+            nc.scalar.activation(
+                out=lk_squares[:],
+                in_=lk[block // PER_PIECE][:, block % PER_PIECE, :],
+                func=ACT.Square,
+                scale=math.sqrt(0.5),
+                accum_out=lk_half_norm[:, block : block + 1],
+            )
+
+        def leave_psum(j, copy):
+            copy(
+                out=lk_grouped[j][:].bitcast(F32).rearrange("p (c n u) -> p c n u", c=PER_PIECE, u=2),
+                in_=lk_t[j][:].rearrange("p (c u n) -> p c n u", c=PER_PIECE, u=2),
+            )
+
+        def quantise_lookup(j):
+            nc.vector.quantize_mx(
+                out=lk_codes[j][:].rearrange("p c n -> p (c n)").bitcast(FP8X4),
+                scales=lk_scales[j][:].rearrange("p c n -> p (c n)"),
+                in_=lk_grouped[j][:],
+            )
+
+        for j in range(PIECES):
+            lk_words = lk[j][:].rearrange("p c d -> p (c d)").bitcast(F32)
+            lk_t.append(psum_plain.tile([P, BANK], F32, tag="plain", name="lk_t%d" % j))
+            for cu in range(PER_PIECE * 2):
+                cols = slice(P * cu, P * (cu + 1))
+                nc.tensor.transpose(lk_t[j][:, cols], lk_words[:, cols], ident[:])
+            half_norm_of(PER_PIECE * j)
+            if j < SCALAR_PIECES:
+                leave_psum(j, nc.scalar.copy)
+            half_norm_of(PER_PIECE * j + 1)
+        for j in range(READY_PIECES):
+            quantise_lookup(j)
 
         emb_t = psum_mx.tile([P, PACK, BATCH], F32)
         for t in range(PACK):
@@ -115,6 +178,8 @@ def tile_privacyloss_s_kernel(tc, x, y, W, lookup, out):
                     start=(g == 0),
                     stop=(g == PASSES - 1),
                 )
+        emb_grouped = keep.tile([P, BATCH, PACK], BF16, align_bytes=64)
+        nc.vector.tensor_copy(out=emb_grouped[:], in_=emb_t[:].rearrange("p t b -> p b t"))
         emb = psum_mx.tile([P, DIM], F32)
         for g in range(PASSES):
             nc.tensor.matmul_mx(
@@ -126,59 +191,25 @@ def tile_privacyloss_s_kernel(tc, x, y, W, lookup, out):
                 start=(g == 0),
                 stop=(g == PASSES - 1),
             )
-        emb_grouped = keep.tile([P, BATCH, PACK], BF16, align_bytes=64)
-        nc.vector.tensor_copy(out=emb_grouped[:], in_=emb_t[:].rearrange("p t b -> p b t"))
         emb_squares = keep.tile([P, DIM], F32)
         emb_norm = keep.tile([P, 1], F32)
         nc.scalar.activation(out=emb_squares[:], in_=emb[:], func=ACT.Square, accum_out=emb_norm[:])
-
-        lk_norm = keep.tile([P, BLOCKS], F32)
-        lk_squares = keep.tile([P, DIM], BF16)
-        lk_codes = []
-        lk_scales = []
-        for j in range(PIECES):
-            for c in range(PER_PIECE):
-                block = PER_PIECE * j + c
-                nc.scalar.activation(
-                    out=lk_squares[:],
-                    in_=lk[j][:, c, :],
-                    func=ACT.Square,
-                    accum_out=lk_norm[:, block : block + 1],
-                )
-            lk_words = lk[j][:].rearrange("p c d -> p (c d)").bitcast(F32)
-            lk_t = psum_plain.tile([P, BANK], F32, tag="plain")
-            for cu in range(PER_PIECE * 2):
-                cols = slice(P * cu, P * (cu + 1))
-                nc.tensor.transpose(lk_t[:, cols], lk_words[:, cols], ident[:])
-            lk_grouped = keep.tile([P, PER_PIECE * P * PACK], BF16, name="lk_grouped%d" % j, align_bytes=64)
-            grouped_words = lk_grouped[:].bitcast(F32).rearrange("p (c n u) -> p c n u", c=PER_PIECE, u=2)
-            transposed_words = lk_t[:].rearrange("p (c u n) -> p c n u", c=PER_PIECE, u=2)
-            if j % 2 == 0:
-                nc.vector.tensor_copy(out=grouped_words, in_=transposed_words)
-            else:
-                nc.scalar.copy(out=grouped_words, in_=transposed_words)
-            lk_codes.append(keep.tile([P, PER_PIECE, P], U32, name="lk_codes%d" % j, align_bytes=64))
-            lk_scales.append(keep.tile([P, PER_PIECE, P], U8, name="lk_scales%d" % j, align_bytes=64))
-            nc.vector.quantize_mx(
-                out=lk_codes[j][:].rearrange("p c n -> p (c n)").bitcast(FP8X4),
-                scales=lk_scales[j][:].rearrange("p c n -> p (c n)"),
-                in_=lk_grouped[:],
-            )
-        lk_half_norm = keep.tile([P, BLOCKS], F32)
-        nc.scalar.mul(out=lk_half_norm[:], in_=lk_norm[:], mul=0.5)
+        diff_norm = keep.tile([P, 1], F32)
+        nc.scalar.activation(out=diff[:], in_=diff[:], func=ACT.Square, accum_out=diff_norm[:])
 
         emb_codes = keep.tile([P, BATCH], U32, align_bytes=64)
         emb_scales = keep.tile([P, BATCH], U8, align_bytes=64)
+        for j in range(SCALAR_PIECES, PIECES):
+            leave_psum(j, nc.vector.tensor_copy)
+        for j in range(READY_PIECES, SCALAR_PIECES):
+            quantise_lookup(j)
         nc.vector.quantize_mx(
             out=emb_codes[:].bitcast(FP8X4),
             scales=emb_scales[:],
             in_=emb_grouped[:].rearrange("p b t -> p (b t)"),
         )
-
-        diff = keep.tile([P, PIXELS], F32)
-        nc.vector.tensor_tensor(out=diff[:], in0=x_sb[:], in1=y_sb[:], op=ALU.subtract)
-        diff_norm = keep.tile([P, 1], F32)
-        nc.scalar.activation(out=diff[:], in_=diff[:], func=ACT.Square, accum_out=diff_norm[:])
+        for j in range(SCALAR_PIECES, PIECES):
+            quantise_lookup(j)
 
         per_bank = BANK // BATCH
         dots = []
@@ -209,11 +240,6 @@ def tile_privacyloss_s_kernel(tc, x, y, W, lookup, out):
                     op0=ALU.subtract, op1=ALU.max,
                 )
 
-        mse_ps = psum_plain.tile([P, BANK], F32, tag="plain")
-        nc.tensor.matmul(out=mse_ps[:, 0:1], lhsT=mean_weight[:], rhs=diff_norm[:], start=True, stop=True)
-        mse = keep.tile([P, 1], F32)
-        nc.scalar.copy(out=mse[:], in_=mse_ps[:, 0:1])
-
         best_t = psum_plain.tile([P, BANK], F32, tag="plain")
         for chain in range(CHAINS):
             nc.tensor.transpose(best_t[:, P * chain : P * (chain + 1)], best[:, chain, :], ident[:])
@@ -221,6 +247,12 @@ def tile_privacyloss_s_kernel(tc, x, y, W, lookup, out):
         nc.vector.tensor_reduce(
             out=top[:], in_=best_t[:, 0 : P * CHAINS], axis=mybir.AxisListType.X, op=ALU.max
         )
+
+        mse_ps = psum_plain.tile([P, BANK], F32, tag="plain")
+        nc.tensor.matmul(out=mse_ps[:, 0:1], lhsT=mean_weight[:], rhs=diff_norm[:], start=True, stop=True)
+        mse = keep.tile([P, 1], F32)
+        nc.vector.tensor_copy(out=mse[:], in_=mse_ps[:, 0:1])
+
         sq_min = keep.tile([P, 1], F32)
         nc.scalar.activation(out=sq_min[:], in_=top[:], func=ACT.Relu, scale=-2.0, bias=emb_norm[:])
         scaled_dist = keep.tile([P, 1], F32)

@@ -27,8 +27,6 @@ PASSES = PIXELS // K_PASS
 BLOCKS = ROWS // P
 PIECES = 4
 PER_PIECE = BLOCKS // PIECES
-SCALAR_PIECES = 3
-READY_PIECES = 2
 CHAINS = 2
 BANK = 512
 
@@ -47,11 +45,11 @@ def tile_privacyloss_s_kernel(tc, x, y, W, lookup, out):
         make_identity(nc, ident[:])
         mean_weight = keep.tile([P, P], F32)
         nc.gpsimd.memset(mean_weight[:], 1.0 / (BATCH * PIXELS))
-        neg_margin = keep.tile([P, 1], F32)
-        nc.vector.memset(neg_margin[:], -MARGIN * SCALE)
         warm = keep.tile([P, 1], F32)
         nc.vector.memset(warm[:], 1.0)
         nc.scalar.activation(out=warm[:], in_=warm[:], func=ACT.Sqrt)
+        neg_ident = keep.tile([P, P], F32)
+        nc.vector.tensor_scalar_mul(out=neg_ident[:], in0=ident[:], scalar1=-1.0)
 
         x_sb = keep.tile([P, PIXELS], BF16)
         y_sb = keep.tile([P, PIXELS], BF16)
@@ -69,29 +67,19 @@ def tile_privacyloss_s_kernel(tc, x, y, W, lookup, out):
                 out=lk[j][:], in_=lookup_rows[:, PER_PIECE * j : PER_PIECE * (j + 1), :]
             )
 
-        nc.sync.dma_start(out=x_sb[:], in_=x.rearrange("b c h w -> b (c h w)"))
         for g in range(PASSES):
+            load_lookup(g)
             nc.sync.dma_start(
                 out=w_raw[g][:].rearrange("p (u e) d -> p u (e d)", u=2), in_=w_rows[g]
             )
-            load_lookup(g)
+        nc.sync.dma_start(out=x_sb[:], in_=x.rearrange("b c h w -> b (c h w)"))
         for j in range(PASSES, PIECES):
             load_lookup(j)
         nc.sync.dma_start(out=y_sb[:], in_=y.rearrange("b c h w -> b (c h w)"))
 
-        x_words = x_sb[:].bitcast(F32)
-        x_t = psum_plain.tile([P, BANK], F32, tag="plain")
-        for gu in range(PASSES * 2):
-            cols = slice(P * gu, P * (gu + 1))
-            nc.tensor.transpose(x_t[:, cols], x_words[:, cols], ident[:])
         x_grouped = keep.tile([P, PASSES * BATCH * PACK], BF16, align_bytes=64)
-        nc.scalar.copy(
-            out=x_grouped[:].bitcast(F32).rearrange("p (g b u) -> p g b u", g=PASSES, u=2),
-            in_=x_t[:].rearrange("p (g u b) -> p g b u", g=PASSES, u=2),
-        )
         x_codes = keep.tile([P, PASSES, BATCH], U32, align_bytes=64)
         x_scales = keep.tile([P, PASSES, BATCH], U8, align_bytes=64)
-
         w_grouped = []
         w_codes = []
         w_scales = []
@@ -99,30 +87,6 @@ def tile_privacyloss_s_kernel(tc, x, y, W, lookup, out):
             w_grouped.append(keep.tile([P, DIM * PACK], BF16, name="w_grouped%d" % g, align_bytes=64))
             w_codes.append(keep.tile([P, DIM], U32, name="w_codes%d" % g, align_bytes=64))
             w_scales.append(keep.tile([P, DIM], U8, name="w_scales%d" % g, align_bytes=64))
-        nc.vector.tensor_copy(
-            out=w_grouped[0][:].rearrange("p (h f i t) -> p h f i t", h=2, f=2, t=PACK),
-            in_=w_raw[0][:].rearrange("p t (h i f) -> p h f i t", h=2, f=2),
-        )
-        nc.vector.quantize_mx(
-            out=x_codes[:].rearrange("p g b -> p (g b)").bitcast(FP8X4),
-            scales=x_scales[:].rearrange("p g b -> p (g b)"),
-            in_=x_grouped[:],
-        )
-        nc.vector.tensor_copy(
-            out=w_grouped[1][:].rearrange("p (h f i t) -> p h f i t", h=2, f=2, t=PACK),
-            in_=w_raw[1][:].rearrange("p t (h i f) -> p h f i t", h=2, f=2),
-        )
-        for g in range(PASSES):
-            nc.vector.quantize_mx(
-                out=w_codes[g][:].bitcast(FP8X4), scales=w_scales[g][:], in_=w_grouped[g][:]
-            )
-
-        diff = keep.tile([P, PIXELS], F32)
-        nc.gpsimd.tensor_tensor(out=diff[:], in0=x_sb[:], in1=y_sb[:], op=ALU.subtract)
-
-        lk_half_norm = keep.tile([P, BLOCKS], F32)
-        lk_squares = keep.tile([P, DIM], BF16)
-        lk_t = []
         lk_grouped = []
         lk_codes = []
         lk_scales = []
@@ -130,6 +94,26 @@ def tile_privacyloss_s_kernel(tc, x, y, W, lookup, out):
             lk_grouped.append(keep.tile([P, PER_PIECE * P * PACK], BF16, name="lk_grouped%d" % j, align_bytes=64))
             lk_codes.append(keep.tile([P, PER_PIECE, P], U32, name="lk_codes%d" % j, align_bytes=64))
             lk_scales.append(keep.tile([P, PER_PIECE, P], U8, name="lk_scales%d" % j, align_bytes=64))
+        emb_grouped = keep.tile([P, BATCH, PACK], BF16, align_bytes=64)
+        emb_codes = keep.tile([P, BATCH], U32, align_bytes=64)
+        emb_scales = keep.tile([P, BATCH], U8, align_bytes=64)
+
+        lk_half_norm = keep.tile([P, BLOCKS], F32)
+        lk_squares = keep.tile([P, DIM], BF16)
+
+        def transpose_words(rows):
+            words = rows.bitcast(F32)
+            bank = psum_plain.tile([P, BANK], F32, tag="plain", name="transposed")
+            for q in range(BANK // P):
+                cols = slice(P * q, P * (q + 1))
+                nc.tensor.transpose(bank[:, cols], words[:, cols], ident[:])
+            return bank
+
+        def pair_words(grouped, bank):
+            nc.scalar.copy(
+                out=grouped[:].bitcast(F32).rearrange("p (a n u) -> p a n u", a=2, u=2),
+                in_=bank[:].rearrange("p (a u n) -> p a n u", a=2, u=2),
+            )
 
         def half_norm_of(block):
             nc.scalar.activation(
@@ -140,11 +124,32 @@ def tile_privacyloss_s_kernel(tc, x, y, W, lookup, out):
                 accum_out=lk_half_norm[:, block : block + 1],
             )
 
-        def leave_psum(j, copy):
-            copy(
-                out=lk_grouped[j][:].bitcast(F32).rearrange("p (c n u) -> p c n u", c=PER_PIECE, u=2),
-                in_=lk_t[j][:].rearrange("p (c u n) -> p c n u", c=PER_PIECE, u=2),
-            )
+        def prepare_lookup(j):
+            bank = transpose_words(lk[j][:].rearrange("p c d -> p (c d)"))
+            half_norm_of(PER_PIECE * j)
+            pair_words(lk_grouped[j], bank)
+            half_norm_of(PER_PIECE * j + 1)
+
+        for j in range(PASSES):
+            prepare_lookup(j)
+        pair_words(x_grouped, transpose_words(x_sb[:]))
+        for j in range(PASSES, PIECES):
+            prepare_lookup(j)
+
+        diff = keep.tile([P, PIXELS], F32)
+        nc.gpsimd.tensor_tensor(out=diff[:], in0=x_sb[:], in1=y_sb[:], op=ALU.subtract)
+
+        def regroup_w(g):
+            sorted_cols = w_grouped[g][:].rearrange("p (h c) -> p h c", h=2)
+            for h in range(2):
+                nc.vector.tensor_copy(
+                    out=sorted_cols[:, h, :].rearrange(
+                        "p (f i1 i2 t) -> p i1 t i2 f", f=2, i2=2, t=PACK
+                    ),
+                    in_=w_raw[g][:, :, (DIM // 2) * h : (DIM // 2) * (h + 1)].rearrange(
+                        "p t (i1 i2 f) -> p i1 t i2 f", i2=2, f=2
+                    ),
+                )
 
         def quantise_lookup(j):
             nc.vector.quantize_mx(
@@ -153,18 +158,19 @@ def tile_privacyloss_s_kernel(tc, x, y, W, lookup, out):
                 in_=lk_grouped[j][:],
             )
 
-        for j in range(PIECES):
-            lk_words = lk[j][:].rearrange("p c d -> p (c d)").bitcast(F32)
-            lk_t.append(psum_plain.tile([P, BANK], F32, tag="plain", name="lk_t%d" % j))
-            for cu in range(PER_PIECE * 2):
-                cols = slice(P * cu, P * (cu + 1))
-                nc.tensor.transpose(lk_t[j][:, cols], lk_words[:, cols], ident[:])
-            half_norm_of(PER_PIECE * j)
-            if j < SCALAR_PIECES:
-                leave_psum(j, nc.scalar.copy)
-            half_norm_of(PER_PIECE * j + 1)
-        for j in range(READY_PIECES):
-            quantise_lookup(j)
+        regroup_w(0)
+        quantise_lookup(0)
+        regroup_w(1)
+        for g in range(PASSES):
+            nc.vector.quantize_mx(
+                out=w_codes[g][:].bitcast(FP8X4), scales=w_scales[g][:], in_=w_grouped[g][:]
+            )
+        nc.vector.quantize_mx(
+            out=x_codes[:].rearrange("p g b -> p (g b)").bitcast(FP8X4),
+            scales=x_scales[:].rearrange("p g b -> p (g b)"),
+            in_=x_grouped[:],
+        )
+        quantise_lookup(1)
 
         emb_t = psum_mx.tile([P, PACK, BATCH], F32)
         for t in range(PACK):
@@ -178,8 +184,15 @@ def tile_privacyloss_s_kernel(tc, x, y, W, lookup, out):
                     start=(g == 0),
                     stop=(g == PASSES - 1),
                 )
-        emb_grouped = keep.tile([P, BATCH, PACK], BF16, align_bytes=64)
         nc.vector.tensor_copy(out=emb_grouped[:], in_=emb_t[:].rearrange("p t b -> p b t"))
+        quantise_lookup(2)
+        nc.vector.quantize_mx(
+            out=emb_codes[:].bitcast(FP8X4),
+            scales=emb_scales[:],
+            in_=emb_grouped[:].rearrange("p b t -> p (b t)"),
+        )
+        quantise_lookup(3)
+
         emb = psum_mx.tile([P, DIM], F32)
         for g in range(PASSES):
             nc.tensor.matmul_mx(
@@ -196,20 +209,6 @@ def tile_privacyloss_s_kernel(tc, x, y, W, lookup, out):
         nc.scalar.activation(out=emb_squares[:], in_=emb[:], func=ACT.Square, accum_out=emb_norm[:])
         diff_norm = keep.tile([P, 1], F32)
         nc.scalar.activation(out=diff[:], in_=diff[:], func=ACT.Square, accum_out=diff_norm[:])
-
-        emb_codes = keep.tile([P, BATCH], U32, align_bytes=64)
-        emb_scales = keep.tile([P, BATCH], U8, align_bytes=64)
-        for j in range(SCALAR_PIECES, PIECES):
-            leave_psum(j, nc.vector.tensor_copy)
-        for j in range(READY_PIECES, SCALAR_PIECES):
-            quantise_lookup(j)
-        nc.vector.quantize_mx(
-            out=emb_codes[:].bitcast(FP8X4),
-            scales=emb_scales[:],
-            in_=emb_grouped[:].rearrange("p b t -> p (b t)"),
-        )
-        for j in range(SCALAR_PIECES, PIECES):
-            quantise_lookup(j)
 
         per_bank = BANK // BATCH
         dots = []
@@ -252,19 +251,22 @@ def tile_privacyloss_s_kernel(tc, x, y, W, lookup, out):
         nc.tensor.matmul(out=mse_ps[:, 0:1], lhsT=mean_weight[:], rhs=diff_norm[:], start=True, stop=True)
         mse = keep.tile([P, 1], F32)
         nc.vector.tensor_copy(out=mse[:], in_=mse_ps[:, 0:1])
+        mse_plus_margin = keep.tile([P, 1], F32)
+        nc.vector.tensor_scalar_add(out=mse_plus_margin[:], in0=mse_ps[:, 0:1], scalar1=MARGIN * SCALE)
 
         sq_min = keep.tile([P, 1], F32)
         nc.scalar.activation(out=sq_min[:], in_=top[:], func=ACT.Relu, scale=-2.0, bias=emb_norm[:])
         scaled_dist = keep.tile([P, 1], F32)
         nc.scalar.activation(out=scaled_dist[:], in_=sq_min[:], func=ACT.Sqrt, scale=SCALE * SCALE)
-        excess = keep.tile([P, 1], F32)
-        nc.scalar.activation(out=excess[:], in_=scaled_dist[:], func=ACT.Relu, bias=neg_margin[:])
 
-        excess_row = psum_plain.tile([P, BANK], F32, tag="plain")
-        nc.tensor.transpose(excess_row[:, 0:P], excess[:].to_broadcast([P, P]), ident[:])
+        neg_dist_row = psum_plain.tile([P, BANK], F32, tag="plain")
+        nc.tensor.matmul(
+            out=neg_dist_row[:, 0:P], lhsT=scaled_dist[:].to_broadcast([P, P]), rhs=neg_ident[:],
+            start=True, stop=True,
+        )
         result = keep.tile([P, BATCH], F32)
         nc.vector.tensor_scalar(
-            out=result[:], in0=excess_row[:, 0:P], scalar1=-1.0, scalar2=mse[:],
-            op0=ALU.mult, op1=ALU.add,
+            out=result[:], in0=neg_dist_row[:, 0:P], scalar1=mse_plus_margin[:], scalar2=mse[:],
+            op0=ALU.add, op1=ALU.min,
         )
         nc.sync.dma_start(out=out.rearrange("(o b) -> o b", o=1), in_=result[0:1, :])

@@ -28,6 +28,7 @@ BLOCKS = ROWS // P
 PIECES = 4
 PER_PIECE = BLOCKS // PIECES
 CHAINS = 2
+HALVES = 2
 BANK = 512
 
 FLOPS = 2 * BATCH * PIXELS * DIM + 2 * BATCH * DIM * ROWS
@@ -91,7 +92,12 @@ def tile_privacyloss_s_kernel(tc, x, y, W, lookup, out):
         lk_codes = []
         lk_scales = []
         for j in range(PIECES):
-            lk_grouped.append(keep.tile([P, PER_PIECE * P * PACK], BF16, name="lk_grouped%d" % j, align_bytes=64))
+            lk_grouped.append(
+                keep.tile(
+                    [P, PER_PIECE * P * PACK], BF16, name="lk_grouped%d" % j, align_bytes=64,
+                    tag="late" if j == PIECES - 1 else "lk_grouped%d" % j,
+                )
+            )
             lk_codes.append(keep.tile([P, PER_PIECE, P], U32, name="lk_codes%d" % j, align_bytes=64))
             lk_scales.append(keep.tile([P, PER_PIECE, P], U8, name="lk_scales%d" % j, align_bytes=64))
         emb_grouped = keep.tile([P, BATCH, PACK], BF16, align_bytes=64)
@@ -135,9 +141,6 @@ def tile_privacyloss_s_kernel(tc, x, y, W, lookup, out):
         pair_words(x_grouped, transpose_words(x_sb[:]))
         for j in range(PASSES, PIECES):
             prepare_lookup(j)
-
-        diff = keep.tile([P, PIXELS], F32)
-        nc.gpsimd.tensor_tensor(out=diff[:], in0=x_sb[:], in1=y_sb[:], op=ALU.subtract)
 
         def regroup_w(g):
             sorted_cols = w_grouped[g][:].rearrange("p (h c) -> p h c", h=2)
@@ -193,6 +196,13 @@ def tile_privacyloss_s_kernel(tc, x, y, W, lookup, out):
         )
         quantise_lookup(3)
 
+        diff = keep.tile([P, HALVES, PIXELS // HALVES], F32, name="diff", align_bytes=64, tag="late")
+        for half in range(HALVES):
+            cols = slice(PIXELS // HALVES * half, PIXELS // HALVES * (half + 1))
+            nc.gpsimd.tensor_tensor(
+                out=diff[:, half, :], in0=x_sb[:, cols], in1=y_sb[:, cols], op=ALU.subtract
+            )
+
         emb = psum_mx.tile([P, DIM], F32)
         for g in range(PASSES):
             nc.tensor.matmul_mx(
@@ -207,8 +217,12 @@ def tile_privacyloss_s_kernel(tc, x, y, W, lookup, out):
         emb_squares = keep.tile([P, DIM], F32)
         emb_norm = keep.tile([P, 1], F32)
         nc.scalar.activation(out=emb_squares[:], in_=emb[:], func=ACT.Square, accum_out=emb_norm[:])
-        diff_norm = keep.tile([P, 1], F32)
-        nc.scalar.activation(out=diff[:], in_=diff[:], func=ACT.Square, accum_out=diff_norm[:])
+        diff_norm = keep.tile([P, HALVES], F32)
+        for half in range(HALVES):
+            nc.scalar.activation(
+                out=diff[:, half, :], in_=diff[:, half, :], func=ACT.Square,
+                accum_out=diff_norm[:, half : half + 1],
+            )
 
         per_bank = BANK // BATCH
         dots = []
@@ -248,7 +262,11 @@ def tile_privacyloss_s_kernel(tc, x, y, W, lookup, out):
         )
 
         mse_ps = psum_plain.tile([P, BANK], F32, tag="plain")
-        nc.tensor.matmul(out=mse_ps[:, 0:1], lhsT=mean_weight[:], rhs=diff_norm[:], start=True, stop=True)
+        for half in range(HALVES):
+            nc.tensor.matmul(
+                out=mse_ps[:, 0:1], lhsT=mean_weight[:], rhs=diff_norm[:, half : half + 1],
+                start=(half == 0), stop=(half == HALVES - 1),
+            )
         mse = keep.tile([P, 1], F32)
         nc.vector.tensor_copy(out=mse[:], in_=mse_ps[:, 0:1])
         mse_plus_margin = keep.tile([P, 1], F32)

@@ -49,8 +49,8 @@ def tile_privacyloss_s_kernel(tc, x, y, W, lookup, out):
         warm = keep.tile([P, 1], F32)
         nc.vector.memset(warm[:], 1.0)
         nc.scalar.activation(out=warm[:], in_=warm[:], func=ACT.Sqrt)
-        neg_ident = keep.tile([P, P], F32)
-        nc.vector.tensor_scalar_mul(out=neg_ident[:], in0=ident[:], scalar1=-1.0)
+        margin_part = keep.tile([P, 1], F32)
+        nc.gpsimd.memset(margin_part[:], MARGIN * SCALE * PIXELS)
 
         x_sb = keep.tile([P, PIXELS], BF16)
         y_sb = keep.tile([P, PIXELS], BF16)
@@ -217,12 +217,19 @@ def tile_privacyloss_s_kernel(tc, x, y, W, lookup, out):
         emb_squares = keep.tile([P, DIM], F32)
         emb_norm = keep.tile([P, 1], F32)
         nc.scalar.activation(out=emb_squares[:], in_=emb[:], func=ACT.Square, accum_out=emb_norm[:])
+        ceiling = keep.tile([P, 1], F32)
+        nc.scalar.activation(
+            out=ceiling[:], in_=emb_norm[:], func=ACT.Copy, scale=0.5, bias=-0.5 * MARGIN * MARGIN
+        )
         diff_norm = keep.tile([P, HALVES], F32)
-        for half in range(HALVES):
+
+        def square_diff(half):
             nc.scalar.activation(
                 out=diff[:, half, :], in_=diff[:, half, :], func=ACT.Square,
                 accum_out=diff_norm[:, half : half + 1],
             )
+
+        square_diff(0)
 
         per_bank = BANK // BATCH
         dots = []
@@ -256,35 +263,29 @@ def tile_privacyloss_s_kernel(tc, x, y, W, lookup, out):
         best_t = psum_plain.tile([P, BANK], F32, tag="plain")
         for chain in range(CHAINS):
             nc.tensor.transpose(best_t[:, P * chain : P * (chain + 1)], best[:, chain, :], ident[:])
+        capped = keep.tile([P, P * CHAINS], F32)
         top = keep.tile([P, 1], F32)
-        nc.vector.tensor_reduce(
-            out=top[:], in_=best_t[:, 0 : P * CHAINS], axis=mybir.AxisListType.X, op=ALU.max
+        nc.vector.tensor_scalar(
+            out=capped[:], in0=best_t[:, 0 : P * CHAINS], scalar1=ceiling[:], scalar2=None,
+            op0=ALU.min, op1=ALU.max, accum_out=top[:],
         )
+        dist = keep.tile([P, 1], F32)
+        nc.scalar.activation(out=dist[:], in_=top[:], func=ACT.Sqrt, scale=-2.0, bias=emb_norm[:])
+        square_diff(1)
 
-        mse_ps = psum_plain.tile([P, BANK], F32, tag="plain")
-        for half in range(HALVES):
+        base = psum_plain.tile([P, BANK], F32, tag="plain")
+        parts = [margin_part[:]] + [diff_norm[:, half : half + 1] for half in range(HALVES)]
+        for part in parts:
             nc.tensor.matmul(
-                out=mse_ps[:, 0:1], lhsT=mean_weight[:], rhs=diff_norm[:, half : half + 1],
-                start=(half == 0), stop=(half == HALVES - 1),
+                out=base[:, 0:1], lhsT=mean_weight[:], rhs=part,
+                start=(part is parts[0]), stop=(part is parts[-1]),
             )
-        mse = keep.tile([P, 1], F32)
-        nc.vector.tensor_copy(out=mse[:], in_=mse_ps[:, 0:1])
-        mse_plus_margin = keep.tile([P, 1], F32)
-        nc.vector.tensor_scalar_add(out=mse_plus_margin[:], in0=mse_ps[:, 0:1], scalar1=MARGIN * SCALE)
 
-        sq_min = keep.tile([P, 1], F32)
-        nc.scalar.activation(out=sq_min[:], in_=top[:], func=ACT.Relu, scale=-2.0, bias=emb_norm[:])
-        scaled_dist = keep.tile([P, 1], F32)
-        nc.scalar.activation(out=scaled_dist[:], in_=sq_min[:], func=ACT.Sqrt, scale=SCALE * SCALE)
-
-        neg_dist_row = psum_plain.tile([P, BANK], F32, tag="plain")
-        nc.tensor.matmul(
-            out=neg_dist_row[:, 0:P], lhsT=scaled_dist[:].to_broadcast([P, P]), rhs=neg_ident[:],
-            start=True, stop=True,
-        )
+        dist_row = psum_plain.tile([P, BANK], F32, tag="plain")
+        nc.tensor.transpose(dist_row[:, 0:P], dist[:].to_broadcast([P, P]), ident[:])
         result = keep.tile([P, BATCH], F32)
         nc.vector.tensor_scalar(
-            out=result[:], in0=neg_dist_row[:, 0:P], scalar1=mse_plus_margin[:], scalar2=mse[:],
-            op0=ALU.add, op1=ALU.min,
+            out=result[:], in0=dist_row[:, 0:P], scalar1=-SCALE, scalar2=base[:, 0:1],
+            op0=ALU.mult, op1=ALU.add,
         )
         nc.sync.dma_start(out=out.rearrange("(o b) -> o b", o=1), in_=result[0:1, :])

@@ -28,7 +28,7 @@ BLOCKS = ROWS // P
 PIECES = 4
 PER_PIECE = BLOCKS // PIECES
 CHAINS = 2
-HALVES = 2
+PE_PIXELS = 384
 BANK = 512
 
 FLOPS = 2 * BATCH * PIXELS * DIM + 2 * BATCH * DIM * ROWS
@@ -49,6 +49,10 @@ def tile_privacyloss_s_kernel(tc, x, y, W, lookup, out):
         warm = keep.tile([P, 1], F32)
         nc.vector.memset(warm[:], 1.0)
         nc.scalar.activation(out=warm[:], in_=warm[:], func=ACT.Sqrt)
+        ident_bf = keep.tile([P, P], BF16)
+        nc.vector.tensor_copy(out=ident_bf[:], in_=ident[:])
+        neg_ident_bf = keep.tile([P, P], BF16)
+        nc.vector.tensor_scalar_mul(out=neg_ident_bf[:], in0=ident[:], scalar1=-1.0)
         margin_part = keep.tile([P, 1], F32)
         nc.gpsimd.memset(margin_part[:], MARGIN * SCALE * PIXELS)
 
@@ -130,17 +134,19 @@ def tile_privacyloss_s_kernel(tc, x, y, W, lookup, out):
                 accum_out=lk_half_norm[:, block : block + 1],
             )
 
-        def prepare_lookup(j):
-            bank = transpose_words(lk[j][:].rearrange("p c d -> p (c d)"))
+        def transposed_lookup(j):
+            return transpose_words(lk[j][:].rearrange("p c d -> p (c d)"))
+
+        for j in range(PASSES):
+            bank = transposed_lookup(j)
             half_norm_of(PER_PIECE * j)
             pair_words(lk_grouped[j], bank)
             half_norm_of(PER_PIECE * j + 1)
-
-        for j in range(PASSES):
-            prepare_lookup(j)
         pair_words(x_grouped, transpose_words(x_sb[:]))
         for j in range(PASSES, PIECES):
-            prepare_lookup(j)
+            pair_words(lk_grouped[j], transposed_lookup(j))
+        for block in range(PASSES * PER_PIECE, BLOCKS):
+            half_norm_of(block)
 
         def regroup_w(g):
             sorted_cols = w_grouped[g][:].rearrange("p (h c) -> p h c", h=2)
@@ -161,47 +167,64 @@ def tile_privacyloss_s_kernel(tc, x, y, W, lookup, out):
                 in_=lk_grouped[j][:],
             )
 
+        def quantise_w(g, h):
+            cols = slice(DIM // 2 * h, DIM // 2 * (h + 1))
+            nc.vector.quantize_mx(
+                out=w_codes[g][:, cols].bitcast(FP8X4),
+                scales=w_scales[g][:, cols],
+                in_=w_grouped[g][:, PACK * DIM // 2 * h : PACK * DIM // 2 * (h + 1)],
+            )
+
+        emb_t = psum_mx.tile([P, PACK, BATCH], F32)
+
+        def first_product(h):
+            for t in (2 * h, 2 * h + 1):
+                for g in range(PASSES):
+                    nc.tensor.matmul_mx(
+                        out=emb_t[:, t, :],
+                        lhsT=w_codes[g][:, P * t : P * (t + 1)].bitcast(FP8X4),
+                        lhsT_scale=w_scales[g][:, P * t : P * (t + 1)],
+                        rhs=x_codes[:, g, :].bitcast(FP8X4),
+                        rhs_scale=x_scales[:, g, :],
+                        start=(g == 0),
+                        stop=(g == PASSES - 1),
+                    )
+
         regroup_w(0)
         quantise_lookup(0)
+        quantise_w(0, 0)
+        quantise_w(0, 1)
         regroup_w(1)
-        for g in range(PASSES):
-            nc.vector.quantize_mx(
-                out=w_codes[g][:].bitcast(FP8X4), scales=w_scales[g][:], in_=w_grouped[g][:]
-            )
+        quantise_w(1, 0)
         nc.vector.quantize_mx(
             out=x_codes[:].rearrange("p g b -> p (g b)").bitcast(FP8X4),
             scales=x_scales[:].rearrange("p g b -> p (g b)"),
             in_=x_grouped[:],
         )
+        first_product(0)
+        quantise_w(1, 1)
+        first_product(1)
         quantise_lookup(1)
-
-        emb_t = psum_mx.tile([P, PACK, BATCH], F32)
-        for t in range(PACK):
-            for g in range(PASSES):
-                nc.tensor.matmul_mx(
-                    out=emb_t[:, t, :],
-                    lhsT=w_codes[g][:, P * t : P * (t + 1)].bitcast(FP8X4),
-                    lhsT_scale=w_scales[g][:, P * t : P * (t + 1)],
-                    rhs=x_codes[:, g, :].bitcast(FP8X4),
-                    rhs_scale=x_scales[:, g, :],
-                    start=(g == 0),
-                    stop=(g == PASSES - 1),
-                )
-        nc.vector.tensor_copy(out=emb_grouped[:], in_=emb_t[:].rearrange("p t b -> p b t"))
         quantise_lookup(2)
+        nc.vector.tensor_copy(out=emb_grouped[:], in_=emb_t[:].rearrange("p t b -> p b t"))
+        quantise_lookup(3)
         nc.vector.quantize_mx(
             out=emb_codes[:].bitcast(FP8X4),
             scales=emb_scales[:],
             in_=emb_grouped[:].rearrange("p b t -> p (b t)"),
         )
-        quantise_lookup(3)
 
-        diff = keep.tile([P, HALVES, PIXELS // HALVES], F32, name="diff", align_bytes=64, tag="late")
-        for half in range(HALVES):
-            cols = slice(PIXELS // HALVES * half, PIXELS // HALVES * (half + 1))
-            nc.gpsimd.tensor_tensor(
-                out=diff[:, half, :], in0=x_sb[:, cols], in1=y_sb[:, cols], op=ALU.subtract
-            )
+        pe_diff = psum_plain.tile([P, BANK], F32, tag="plain")
+        nc.tensor.matmul(
+            out=pe_diff[:, 0:PE_PIXELS], lhsT=ident_bf[:], rhs=x_sb[:, 0:PE_PIXELS], start=True, stop=False
+        )
+        nc.tensor.matmul(
+            out=pe_diff[:, 0:PE_PIXELS], lhsT=neg_ident_bf[:], rhs=y_sb[:, 0:PE_PIXELS], start=False, stop=True
+        )
+        diff = keep.tile([P, PIXELS - PE_PIXELS], F32, name="diff", align_bytes=64, tag="late")
+        nc.gpsimd.tensor_tensor(
+            out=diff[:], in0=x_sb[:, PE_PIXELS:PIXELS], in1=y_sb[:, PE_PIXELS:PIXELS], op=ALU.subtract
+        )
 
         emb = psum_mx.tile([P, DIM], F32)
         for g in range(PASSES):
@@ -221,23 +244,20 @@ def tile_privacyloss_s_kernel(tc, x, y, W, lookup, out):
         nc.scalar.activation(
             out=ceiling[:], in_=emb_norm[:], func=ACT.Copy, scale=0.5, bias=-0.5 * MARGIN * MARGIN
         )
-        diff_norm = keep.tile([P, HALVES], F32)
+        diff_norm = keep.tile([P, 2], F32)
+        pe_squares = keep.tile([P, PE_PIXELS], F32)
+        for i, (squares, part) in enumerate(((pe_squares[:], pe_diff[:, 0:PE_PIXELS]), (diff[:], diff[:]))):
+            nc.scalar.activation(out=squares, in_=part, func=ACT.Square, accum_out=diff_norm[:, i : i + 1])
 
-        def square_diff(half):
-            nc.scalar.activation(
-                out=diff[:, half, :], in_=diff[:, half, :], func=ACT.Square,
-                accum_out=diff_norm[:, half : half + 1],
-            )
-
-        square_diff(0)
-
-        per_bank = BANK // BATCH
         dots = []
-        for half in range(BLOCKS // per_bank):
-            dots.append(psum_mx.tile([P, per_bank, BATCH], F32, name="dots%d" % half))
+        for block in range(CHAINS):
+            dots.append(psum_mx.tile([P, BATCH], F32, name="dots%d" % block)[:])
+        for pair in range((BLOCKS - CHAINS) // 2):
+            bank = psum_plain.tile([P, BANK], F32, tag="plain", name="dots")
+            dots.extend([bank[:, 0:BATCH], bank[:, BATCH : 2 * BATCH]])
         for block in range(BLOCKS):
             nc.tensor.matmul_mx(
-                out=dots[block // per_bank][:, block % per_bank, :],
+                out=dots[block],
                 lhsT=lk_codes[block // PER_PIECE][:, block % PER_PIECE, :].bitcast(FP8X4),
                 lhsT_scale=lk_scales[block // PER_PIECE][:, block % PER_PIECE, :],
                 rhs=emb_codes[:].bitcast(FP8X4),
@@ -248,7 +268,7 @@ def tile_privacyloss_s_kernel(tc, x, y, W, lookup, out):
         best = keep.tile([P, CHAINS, BATCH], F32)
         for block in range(BLOCKS):
             running = best[:, block % CHAINS, :]
-            scores = dots[block // per_bank][:, block % per_bank, :]
+            scores = dots[block]
             half_norm = lk_half_norm[:, block : block + 1]
             if block < CHAINS:
                 nc.vector.tensor_scalar(
@@ -271,10 +291,9 @@ def tile_privacyloss_s_kernel(tc, x, y, W, lookup, out):
         )
         dist = keep.tile([P, 1], F32)
         nc.scalar.activation(out=dist[:], in_=top[:], func=ACT.Sqrt, scale=-2.0, bias=emb_norm[:])
-        square_diff(1)
 
         base = psum_plain.tile([P, BANK], F32, tag="plain")
-        parts = [margin_part[:]] + [diff_norm[:, half : half + 1] for half in range(HALVES)]
+        parts = [margin_part[:], diff_norm[:, 0:1], diff_norm[:, 1:2]]
         for part in parts:
             nc.tensor.matmul(
                 out=base[:, 0:1], lhsT=mean_weight[:], rhs=part,

@@ -29,6 +29,8 @@ PIECES = 4
 PER_PIECE = BLOCKS // PIECES
 CHAINS = 2
 PE_PIXELS = 384
+SCALAR_PIXELS = 384
+SQUARE = 32
 BANK = 512
 
 FLOPS = 2 * BATCH * PIXELS * DIM + 2 * BATCH * DIM * ROWS
@@ -53,8 +55,10 @@ def tile_privacyloss_s_kernel(tc, x, y, W, lookup, out):
         nc.vector.tensor_copy(out=ident_bf[:], in_=ident[:])
         neg_ident_bf = keep.tile([P, P], BF16)
         nc.vector.tensor_scalar_mul(out=neg_ident_bf[:], in0=ident[:], scalar1=-1.0)
-        margin_part = keep.tile([P, 1], F32)
-        nc.gpsimd.memset(margin_part[:], MARGIN * SCALE * PIXELS)
+        diff_norm = keep.tile([P, 4], F32)
+        nc.gpsimd.memset(diff_norm[:, 3:4], MARGIN * SCALE * PIXELS)
+        column = keep.tile([P, SQUARE], F32, align_bytes=64)
+        nc.gpsimd.memset(column[:], 0.0)
 
         x_sb = keep.tile([P, PIXELS], BF16)
         y_sb = keep.tile([P, PIXELS], BF16)
@@ -64,7 +68,7 @@ def tile_privacyloss_s_kernel(tc, x, y, W, lookup, out):
         lk = []
         for j in range(PIECES):
             lk.append(keep.tile([P, PER_PIECE, DIM], BF16, name="lk%d" % j))
-        w_rows = W.rearrange("(g u p e) d -> g p u (e d)", g=PASSES, u=2, e=2)
+        w_rows = W.rearrange("(g p t) d -> g p t d", g=PASSES, t=PACK)
         lookup_rows = lookup.rearrange("(p c) d -> p c d", c=BLOCKS)
 
         def load_lookup(j):
@@ -72,12 +76,14 @@ def tile_privacyloss_s_kernel(tc, x, y, W, lookup, out):
                 out=lk[j][:], in_=lookup_rows[:, PER_PIECE * j : PER_PIECE * (j + 1), :]
             )
 
-        for g in range(PASSES):
-            load_lookup(g)
-            nc.sync.dma_start(
-                out=w_raw[g][:].rearrange("p (u e) d -> p u (e d)", u=2), in_=w_rows[g]
-            )
+        def load_w(g):
+            nc.sync.dma_start(out=w_raw[g][:], in_=w_rows[g])
+
+        load_lookup(0)
+        load_w(0)
+        load_lookup(1)
         nc.sync.dma_start(out=x_sb[:], in_=x.rearrange("b c h w -> b (c h w)"))
+        load_w(1)
         for j in range(PASSES, PIECES):
             load_lookup(j)
         nc.sync.dma_start(out=y_sb[:], in_=y.rearrange("b c h w -> b (c h w)"))
@@ -109,14 +115,19 @@ def tile_privacyloss_s_kernel(tc, x, y, W, lookup, out):
         emb_scales = keep.tile([P, BATCH], U8, align_bytes=64)
 
         lk_half_norm = keep.tile([P, BLOCKS], F32)
+        lk_half_norm_1 = keep.tile([P, 1], F32)
         lk_squares = keep.tile([P, DIM], BF16)
 
         def transpose_words(rows):
             words = rows.bitcast(F32)
             bank = psum_plain.tile([P, BANK], F32, tag="plain", name="transposed")
-            for q in range(BANK // P):
-                cols = slice(P * q, P * (q + 1))
-                nc.tensor.transpose(bank[:, cols], words[:, cols], ident[:])
+            for a in range(2):
+                for u in range(2):
+                    nc.tensor.transpose(
+                        bank[:, P * (2 * a + u) : P * (2 * a + u + 1)],
+                        words[:, 2 * P * a + u : 2 * P * (a + 1) : 2],
+                        ident[:],
+                    )
             return bank
 
         def pair_words(grouped, bank):
@@ -137,28 +148,30 @@ def tile_privacyloss_s_kernel(tc, x, y, W, lookup, out):
         def transposed_lookup(j):
             return transpose_words(lk[j][:].rearrange("p c d -> p (c d)"))
 
-        for j in range(PASSES):
-            bank = transposed_lookup(j)
-            half_norm_of(PER_PIECE * j)
-            pair_words(lk_grouped[j], bank)
-            half_norm_of(PER_PIECE * j + 1)
+        bank = transposed_lookup(0)
+        half_norm_of(0)
+        pair_words(lk_grouped[0], bank)
+        bank = transposed_lookup(1)
+        half_norm_of(2)
+        pair_words(lk_grouped[1], bank)
         pair_words(x_grouped, transpose_words(x_sb[:]))
+        half_norm_of(3)
         for j in range(PASSES, PIECES):
             pair_words(lk_grouped[j], transposed_lookup(j))
         for block in range(PASSES * PER_PIECE, BLOCKS):
             half_norm_of(block)
+        vector_squares = keep.tile([P, DIM], F32)
+        block_1 = lk[0][:, 1, :]
+        nc.vector.scalar_tensor_tensor(
+            out=vector_squares[:], in0=block_1, scalar=0.5, in1=block_1,
+            op0=ALU.mult, op1=ALU.mult, accum_out=lk_half_norm_1[:],
+        )
 
         def regroup_w(g):
-            sorted_cols = w_grouped[g][:].rearrange("p (h c) -> p h c", h=2)
-            for h in range(2):
-                nc.vector.tensor_copy(
-                    out=sorted_cols[:, h, :].rearrange(
-                        "p (f i1 i2 t) -> p i1 t i2 f", f=2, i2=2, t=PACK
-                    ),
-                    in_=w_raw[g][:, :, (DIM // 2) * h : (DIM // 2) * (h + 1)].rearrange(
-                        "p t (i1 i2 f) -> p i1 t i2 f", i2=2, f=2
-                    ),
-                )
+            nc.vector.tensor_copy(
+                out=w_grouped[g][:].rearrange("p (s i t) -> p i t s", s=PACK, t=PACK),
+                in_=w_raw[g][:].rearrange("p t (i s) -> p i t s", s=PACK),
+            )
 
         def quantise_lookup(j):
             nc.vector.quantize_mx(
@@ -195,12 +208,12 @@ def tile_privacyloss_s_kernel(tc, x, y, W, lookup, out):
         quantise_w(0, 0)
         quantise_w(0, 1)
         regroup_w(1)
-        quantise_w(1, 0)
         nc.vector.quantize_mx(
             out=x_codes[:].rearrange("p g b -> p (g b)").bitcast(FP8X4),
             scales=x_scales[:].rearrange("p g b -> p (g b)"),
             in_=x_grouped[:],
         )
+        quantise_w(1, 0)
         first_product(0)
         quantise_w(1, 1)
         first_product(1)
@@ -237,6 +250,13 @@ def tile_privacyloss_s_kernel(tc, x, y, W, lookup, out):
                 start=(g == 0),
                 stop=(g == PASSES - 1),
             )
+        pe_squares = keep.tile([P, PE_PIXELS], F32)
+        nc.scalar.activation(
+            out=pe_squares[:], in_=pe_diff[:, 0:PE_PIXELS], func=ACT.Square, accum_out=diff_norm[:, 0:1]
+        )
+        first, last = diff[:, 0:SCALAR_PIXELS], diff[:, SCALAR_PIXELS:]
+        nc.scalar.activation(out=first, in_=first, func=ACT.Square, accum_out=diff_norm[:, 1:2])
+
         emb_squares = keep.tile([P, DIM], F32)
         emb_norm = keep.tile([P, 1], F32)
         nc.scalar.activation(out=emb_squares[:], in_=emb[:], func=ACT.Square, accum_out=emb_norm[:])
@@ -244,10 +264,6 @@ def tile_privacyloss_s_kernel(tc, x, y, W, lookup, out):
         nc.scalar.activation(
             out=ceiling[:], in_=emb_norm[:], func=ACT.Copy, scale=0.5, bias=-0.5 * MARGIN * MARGIN
         )
-        diff_norm = keep.tile([P, 2], F32)
-        pe_squares = keep.tile([P, PE_PIXELS], F32)
-        for i, (squares, part) in enumerate(((pe_squares[:], pe_diff[:, 0:PE_PIXELS]), (diff[:], diff[:]))):
-            nc.scalar.activation(out=squares, in_=part, func=ACT.Square, accum_out=diff_norm[:, i : i + 1])
 
         dots = []
         for block in range(CHAINS):
@@ -269,7 +285,7 @@ def tile_privacyloss_s_kernel(tc, x, y, W, lookup, out):
         for block in range(BLOCKS):
             running = best[:, block % CHAINS, :]
             scores = dots[block]
-            half_norm = lk_half_norm[:, block : block + 1]
+            half_norm = lk_half_norm_1[:] if block == 1 else lk_half_norm[:, block : block + 1]
             if block < CHAINS:
                 nc.vector.tensor_scalar(
                     out=running, in0=scores, scalar1=half_norm, scalar2=None, op0=ALU.subtract
@@ -279,6 +295,10 @@ def tile_privacyloss_s_kernel(tc, x, y, W, lookup, out):
                     out=running, in0=scores, scalar=half_norm, in1=running,
                     op0=ALU.subtract, op1=ALU.max,
                 )
+
+        nc.vector.scalar_tensor_tensor(
+            out=last, in0=last, scalar=1.0, in1=last, op0=ALU.mult, op1=ALU.mult, accum_out=diff_norm[:, 2:3]
+        )
 
         best_t = psum_plain.tile([P, BANK], F32, tag="plain")
         for chain in range(CHAINS):
@@ -292,19 +312,15 @@ def tile_privacyloss_s_kernel(tc, x, y, W, lookup, out):
         dist = keep.tile([P, 1], F32)
         nc.scalar.activation(out=dist[:], in_=top[:], func=ACT.Sqrt, scale=-2.0, bias=emb_norm[:])
 
-        base = psum_plain.tile([P, BANK], F32, tag="plain")
-        parts = [margin_part[:], diff_norm[:, 0:1], diff_norm[:, 1:2]]
-        for part in parts:
-            nc.tensor.matmul(
-                out=base[:, 0:1], lhsT=mean_weight[:], rhs=part,
-                start=(part is parts[0]), stop=(part is parts[-1]),
-            )
+        sums = psum_plain.tile([P, 4], F32, tag="plain", name="sums")
+        nc.tensor.matmul(out=sums[:], lhsT=mean_weight[:], rhs=diff_norm[:], start=True, stop=True)
+        base = keep.tile([P, 1], F32)
+        nc.vector.tensor_reduce(out=base[:], in_=sums[:], axis=mybir.AxisListType.X, op=ALU.add)
 
-        dist_row = psum_plain.tile([P, BANK], F32, tag="plain")
-        nc.tensor.transpose(dist_row[:, 0:P], dist[:].to_broadcast([P, P]), ident[:])
-        result = keep.tile([P, BATCH], F32)
         nc.vector.tensor_scalar(
-            out=result[:], in0=dist_row[:, 0:P], scalar1=-SCALE, scalar2=base[:, 0:1],
+            out=column[:, 0:1], in0=dist[:], scalar1=-SCALE, scalar2=base[:],
             op0=ALU.mult, op1=ALU.add,
         )
-        nc.sync.dma_start(out=out.rearrange("(o b) -> o b", o=1), in_=result[0:1, :])
+        rows = keep.tile([P, SQUARE], F32, align_bytes=64)
+        nc.vector.transpose(out=rows[:], in_=column[:])
+        nc.sync.dma_start(out=out.rearrange("(q b) -> q b", b=SQUARE), in_=rows[0:P:SQUARE, :])

@@ -118,14 +118,15 @@ def tile_privacyloss_s_kernel(tc, x, y, W, lookup, out):
         lk_half_norm_1 = keep.tile([P, 1], F32)
         lk_squares = keep.tile([P, DIM], BF16)
 
-        def transpose_words(rows):
-            words = rows.bitcast(F32)
+        def transpose_words(rows, step):
+            words = rows.bitcast(F32).rearrange("p (a w) -> p a w", a=2)
             bank = psum_plain.tile([P, BANK], F32, tag="plain", name="transposed")
             for a in range(2):
                 for u in range(2):
+                    start = u if step == 2 else P * u
                     nc.tensor.transpose(
                         bank[:, P * (2 * a + u) : P * (2 * a + u + 1)],
-                        words[:, 2 * P * a + u : 2 * P * (a + 1) : 2],
+                        words[:, a, start : start + step * (P - 1) + 1 : step],
                         ident[:],
                     )
             return bank
@@ -146,7 +147,7 @@ def tile_privacyloss_s_kernel(tc, x, y, W, lookup, out):
             )
 
         def transposed_lookup(j):
-            return transpose_words(lk[j][:].rearrange("p c d -> p (c d)"))
+            return transpose_words(lk[j][:].rearrange("p c d -> p (c d)"), 1)
 
         bank = transposed_lookup(0)
         half_norm_of(0)
@@ -154,7 +155,7 @@ def tile_privacyloss_s_kernel(tc, x, y, W, lookup, out):
         bank = transposed_lookup(1)
         half_norm_of(2)
         pair_words(lk_grouped[1], bank)
-        pair_words(x_grouped, transpose_words(x_sb[:]))
+        pair_words(x_grouped, transpose_words(x_sb[:], 2))
         half_norm_of(3)
         for j in range(PASSES, PIECES):
             pair_words(lk_grouped[j], transposed_lookup(j))
@@ -168,10 +169,16 @@ def tile_privacyloss_s_kernel(tc, x, y, W, lookup, out):
         )
 
         def regroup_w(g):
-            nc.vector.tensor_copy(
-                out=w_grouped[g][:].rearrange("p (s i t) -> p i t s", s=PACK, t=PACK),
-                in_=w_raw[g][:].rearrange("p t (i s) -> p i t s", s=PACK),
-            )
+            sorted_cols = w_grouped[g][:].rearrange("p (h c) -> p h c", h=2)
+            for h in range(2):
+                nc.vector.tensor_copy(
+                    out=sorted_cols[:, h, :].rearrange(
+                        "p (f i1 i2 t) -> p i1 t i2 f", f=2, i2=2, t=PACK
+                    ),
+                    in_=w_raw[g][:, :, (DIM // 2) * h : (DIM // 2) * (h + 1)].rearrange(
+                        "p t (i1 i2 f) -> p i1 t i2 f", i2=2, f=2
+                    ),
+                )
 
         def quantise_lookup(j):
             nc.vector.quantize_mx(

@@ -169,16 +169,10 @@ def tile_privacyloss_s_kernel(tc, x, y, W, lookup, out):
         )
 
         def regroup_w(g):
-            sorted_cols = w_grouped[g][:].rearrange("p (h c) -> p h c", h=2)
-            for h in range(2):
-                nc.vector.tensor_copy(
-                    out=sorted_cols[:, h, :].rearrange(
-                        "p (f i1 i2 t) -> p i1 t i2 f", f=2, i2=2, t=PACK
-                    ),
-                    in_=w_raw[g][:, :, (DIM // 2) * h : (DIM // 2) * (h + 1)].rearrange(
-                        "p t (i1 i2 f) -> p i1 t i2 f", i2=2, f=2
-                    ),
-                )
+            nc.vector.tensor_copy(
+                out=w_grouped[g][:].rearrange("p (f n m t) -> p n t m f", f=2, m=2, t=PACK),
+                in_=w_raw[g][:].rearrange("p t (n m f) -> p n t m f", m=2, f=2),
+            )
 
         def quantise_lookup(j):
             nc.vector.quantize_mx(
@@ -187,23 +181,23 @@ def tile_privacyloss_s_kernel(tc, x, y, W, lookup, out):
                 in_=lk_grouped[j][:],
             )
 
-        def quantise_w(g, h):
-            cols = slice(DIM // 2 * h, DIM // 2 * (h + 1))
+        def quantise_w(g, first, end):
             nc.vector.quantize_mx(
-                out=w_codes[g][:, cols].bitcast(FP8X4),
-                scales=w_scales[g][:, cols],
-                in_=w_grouped[g][:, PACK * DIM // 2 * h : PACK * DIM // 2 * (h + 1)],
+                out=w_codes[g][:, first:end].bitcast(FP8X4),
+                scales=w_scales[g][:, first:end],
+                in_=w_grouped[g][:, PACK * first : PACK * end],
             )
 
-        emb_t = psum_mx.tile([P, PACK, BATCH], F32)
+        emb_t = psum_mx.tile([P, 2, 2, BATCH], F32)
 
-        def first_product(h):
-            for t in (2 * h, 2 * h + 1):
+        def first_product(f):
+            for h in range(2):
+                cols = slice(P * (2 * f + h), P * (2 * f + h + 1))
                 for g in range(PASSES):
                     nc.tensor.matmul_mx(
-                        out=emb_t[:, t, :],
-                        lhsT=w_codes[g][:, P * t : P * (t + 1)].bitcast(FP8X4),
-                        lhsT_scale=w_scales[g][:, P * t : P * (t + 1)],
+                        out=emb_t[:, f, h, :],
+                        lhsT=w_codes[g][:, cols].bitcast(FP8X4),
+                        lhsT_scale=w_scales[g][:, cols],
                         rhs=x_codes[:, g, :].bitcast(FP8X4),
                         rhs_scale=x_scales[:, g, :],
                         start=(g == 0),
@@ -212,21 +206,23 @@ def tile_privacyloss_s_kernel(tc, x, y, W, lookup, out):
 
         regroup_w(0)
         quantise_lookup(0)
-        quantise_w(0, 0)
-        quantise_w(0, 1)
+        quantise_w(0, 0, DIM)
         regroup_w(1)
         nc.vector.quantize_mx(
             out=x_codes[:].rearrange("p g b -> p (g b)").bitcast(FP8X4),
             scales=x_scales[:].rearrange("p g b -> p (g b)"),
             in_=x_grouped[:],
         )
-        quantise_w(1, 0)
+        quantise_w(1, 0, DIM // 2)
         first_product(0)
-        quantise_w(1, 1)
+        quantise_w(1, DIM // 2, DIM)
         first_product(1)
         quantise_lookup(1)
         quantise_lookup(2)
-        nc.vector.tensor_copy(out=emb_grouped[:], in_=emb_t[:].rearrange("p t b -> p b t"))
+        nc.vector.tensor_copy(
+            out=emb_grouped[:].rearrange("p b (h f) -> p b h f", h=2),
+            in_=emb_t[:].rearrange("p f h b -> p b h f"),
+        )
         quantise_lookup(3)
         nc.vector.quantize_mx(
             out=emb_codes[:].bitcast(FP8X4),

import math
from contextlib import ExitStack

import concourse.mybir as mybir
from concourse.masks import make_identity

F32 = mybir.dt.float32
BF16 = mybir.dt.bfloat16
U32 = mybir.dt.uint32
U8 = mybir.dt.uint8
FP8X4 = mybir.dt.float8_e4m3fn_x4
ACT = mybir.ActivationFunctionType
ALU = mybir.AluOpType

P = 128
PACK = 4
K_PASS = P * PACK

BATCH = 128
PIXELS = 1024
DIM = 512
ROWS = 1024
MARGIN = 50.0
SCALE = 5.0

PASSES = PIXELS // K_PASS
BLOCKS = ROWS // P
PIECES = 4
PER_PIECE = BLOCKS // PIECES
CHAINS = 2
PE_PIXELS = 384
SCALAR_PIXELS = 384
SQUARE = 32
BANK = 512

FLOPS = 2 * BATCH * PIXELS * DIM + 2 * BATCH * DIM * ROWS


def tile_privacyloss_s_kernel(tc, x, y, W, lookup, out):
    nc = tc.nc
    with ExitStack() as ctx:
        keep = ctx.enter_context(tc.tile_pool(name="keep", bufs=1))
        psum_plain = ctx.enter_context(tc.psum_pool(name="psum_plain", bufs=4))
        psum_mx = ctx.enter_context(tc.psum_pool(name="psum_mx", bufs=1))
        ctx.enter_context(tc.manual_schedule())

        ident = keep.tile([P, P], F32)
        make_identity(nc, ident[:])
        mean_weight = keep.tile([P, P], F32)
        nc.gpsimd.memset(mean_weight[:], 1.0 / (BATCH * PIXELS))
        warm = keep.tile([P, 1], F32)
        nc.vector.memset(warm[:], 1.0)
        nc.scalar.activation(out=warm[:], in_=warm[:], func=ACT.Sqrt)
        ident_bf = keep.tile([P, P], BF16)
        nc.vector.tensor_copy(out=ident_bf[:], in_=ident[:])
        neg_ident_bf = keep.tile([P, P], BF16)
        nc.vector.tensor_scalar_mul(out=neg_ident_bf[:], in0=ident[:], scalar1=-1.0)
        diff_norm = keep.tile([P, 4], F32)
        nc.gpsimd.memset(diff_norm[:, 3:4], MARGIN * SCALE * PIXELS)
        column = keep.tile([P, SQUARE], F32, align_bytes=64)
        nc.gpsimd.memset(column[:], 0.0)

        x_sb = keep.tile([P, PIXELS], BF16)
        y_sb = keep.tile([P, PIXELS], BF16)
        w_raw = []
        for g in range(PASSES):
            w_raw.append(keep.tile([P, PACK, DIM], BF16, name="w_raw%d" % g))
        lk = []
        for j in range(PIECES):
            lk.append(keep.tile([P, PER_PIECE, DIM], BF16, name="lk%d" % j))
        w_rows = W.rearrange("(g p t) d -> g p t d", g=PASSES, t=PACK)
        lookup_rows = lookup.rearrange("(p c) d -> p c d", c=BLOCKS)

        def load_lookup(j):
            nc.sync.dma_start(
                out=lk[j][:], in_=lookup_rows[:, PER_PIECE * j : PER_PIECE * (j + 1), :]
            )

        def load_w(g):
            nc.sync.dma_start(out=w_raw[g][:], in_=w_rows[g])

        load_lookup(0)
        load_w(0)
        load_lookup(1)
        nc.sync.dma_start(out=x_sb[:], in_=x.rearrange("b c h w -> b (c h w)"))
        load_w(1)
        for j in range(PASSES, PIECES):
            load_lookup(j)
        nc.sync.dma_start(out=y_sb[:], in_=y.rearrange("b c h w -> b (c h w)"))

        x_grouped = keep.tile([P, PASSES * BATCH * PACK], BF16, align_bytes=64)
        x_codes = keep.tile([P, PASSES, BATCH], U32, align_bytes=64)
        x_scales = keep.tile([P, PASSES, BATCH], U8, align_bytes=64)
        w_grouped = []
        w_codes = []
        w_scales = []
        for g in range(PASSES):
            w_grouped.append(keep.tile([P, DIM * PACK], BF16, name="w_grouped%d" % g, align_bytes=64))
            w_codes.append(keep.tile([P, DIM], U32, name="w_codes%d" % g, align_bytes=64))
            w_scales.append(keep.tile([P, DIM], U8, name="w_scales%d" % g, align_bytes=64))
        lk_grouped = []
        lk_codes = []
        lk_scales = []
        for j in range(PIECES):
            lk_grouped.append(
                keep.tile(
                    [P, PER_PIECE * P * PACK], BF16, name="lk_grouped%d" % j, align_bytes=64,
                    tag="late" if j == PIECES - 1 else "lk_grouped%d" % j,
                )
            )
            lk_codes.append(keep.tile([P, PER_PIECE, P], U32, name="lk_codes%d" % j, align_bytes=64))
            lk_scales.append(keep.tile([P, PER_PIECE, P], U8, name="lk_scales%d" % j, align_bytes=64))
        emb_grouped = keep.tile([P, BATCH, PACK], BF16, align_bytes=64)
        emb_codes = keep.tile([P, BATCH], U32, align_bytes=64)
        emb_scales = keep.tile([P, BATCH], U8, align_bytes=64)

        lk_half_norm = keep.tile([P, BLOCKS], F32)
        lk_half_norm_1 = keep.tile([P, 1], F32)
        lk_squares = keep.tile([P, DIM], BF16)

        def transpose_words(rows, step):
            words = rows.bitcast(F32).rearrange("p (a w) -> p a w", a=2)
            bank = psum_plain.tile([P, BANK], F32, tag="plain", name="transposed")
            for a in range(2):
                for u in range(2):
                    start = u if step == 2 else P * u
                    nc.tensor.transpose(
                        bank[:, P * (2 * a + u) : P * (2 * a + u + 1)],
                        words[:, a, start : start + step * (P - 1) + 1 : step],
                        ident[:],
                    )
            return bank

        def pair_words(grouped, bank):
            nc.scalar.copy(
                out=grouped[:].bitcast(F32).rearrange("p (a n u) -> p a n u", a=2, u=2),
                in_=bank[:].rearrange("p (a u n) -> p a n u", a=2, u=2),
            )

        def half_norm_of(block):
            nc.scalar.activation(
                out=lk_squares[:],
                in_=lk[block // PER_PIECE][:, block % PER_PIECE, :],
                func=ACT.Square,
                scale=math.sqrt(0.5),
                accum_out=lk_half_norm[:, block : block + 1],
            )

        def transposed_lookup(j):
            return transpose_words(lk[j][:].rearrange("p c d -> p (c d)"), 1)

        bank = transposed_lookup(0)
        half_norm_of(0)
        pair_words(lk_grouped[0], bank)
        bank = transposed_lookup(1)
        half_norm_of(2)
        pair_words(lk_grouped[1], bank)
        pair_words(x_grouped, transpose_words(x_sb[:], 2))
        half_norm_of(3)
        for j in range(PASSES, PIECES):
            pair_words(lk_grouped[j], transposed_lookup(j))
        for block in range(PASSES * PER_PIECE, BLOCKS):
            half_norm_of(block)
        vector_squares = keep.tile([P, DIM], F32)
        block_1 = lk[0][:, 1, :]
        nc.vector.scalar_tensor_tensor(
            out=vector_squares[:], in0=block_1, scalar=0.5, in1=block_1,
            op0=ALU.mult, op1=ALU.mult, accum_out=lk_half_norm_1[:],
        )

        def regroup_w(g):
            nc.vector.tensor_copy(
                out=w_grouped[g][:].rearrange("p (f n m t) -> p n t m f", f=2, m=2, t=PACK),
                in_=w_raw[g][:].rearrange("p t (n m f) -> p n t m f", m=2, f=2),
            )

        def quantise_lookup(j):
            nc.vector.quantize_mx(
                out=lk_codes[j][:].rearrange("p c n -> p (c n)").bitcast(FP8X4),
                scales=lk_scales[j][:].rearrange("p c n -> p (c n)"),
                in_=lk_grouped[j][:],
            )

        def quantise_w(g, first, end):
            nc.vector.quantize_mx(
                out=w_codes[g][:, first:end].bitcast(FP8X4),
                scales=w_scales[g][:, first:end],
                in_=w_grouped[g][:, PACK * first : PACK * end],
            )

        emb_t = psum_mx.tile([P, 2, 2, BATCH], F32)

        def first_product(f):
            for h in range(2):
                cols = slice(P * (2 * f + h), P * (2 * f + h + 1))
                for g in range(PASSES):
                    nc.tensor.matmul_mx(
                        out=emb_t[:, f, h, :],
                        lhsT=w_codes[g][:, cols].bitcast(FP8X4),
                        lhsT_scale=w_scales[g][:, cols],
                        rhs=x_codes[:, g, :].bitcast(FP8X4),
                        rhs_scale=x_scales[:, g, :],
                        start=(g == 0),
                        stop=(g == PASSES - 1),
                    )

        regroup_w(0)
        quantise_lookup(0)
        quantise_w(0, 0, DIM)
        regroup_w(1)
        nc.vector.quantize_mx(
            out=x_codes[:].rearrange("p g b -> p (g b)").bitcast(FP8X4),
            scales=x_scales[:].rearrange("p g b -> p (g b)"),
            in_=x_grouped[:],
        )
        quantise_w(1, 0, DIM // 2)
        first_product(0)
        quantise_w(1, DIM // 2, DIM)
        first_product(1)
        quantise_lookup(1)
        quantise_lookup(2)
        nc.vector.tensor_copy(
            out=emb_grouped[:].rearrange("p b (h f) -> p b h f", h=2),
            in_=emb_t[:].rearrange("p f h b -> p b h f"),
        )
        quantise_lookup(3)
        nc.vector.quantize_mx(
            out=emb_codes[:].bitcast(FP8X4),
            scales=emb_scales[:],
            in_=emb_grouped[:].rearrange("p b t -> p (b t)"),
        )

        pe_diff = psum_plain.tile([P, BANK], F32, tag="plain")
        nc.tensor.matmul(
            out=pe_diff[:, 0:PE_PIXELS], lhsT=ident_bf[:], rhs=x_sb[:, 0:PE_PIXELS], start=True, stop=False
        )
        nc.tensor.matmul(
            out=pe_diff[:, 0:PE_PIXELS], lhsT=neg_ident_bf[:], rhs=y_sb[:, 0:PE_PIXELS], start=False, stop=True
        )
        diff = keep.tile([P, PIXELS - PE_PIXELS], F32, name="diff", align_bytes=64, tag="late")
        nc.gpsimd.tensor_tensor(
            out=diff[:], in0=x_sb[:, PE_PIXELS:PIXELS], in1=y_sb[:, PE_PIXELS:PIXELS], op=ALU.subtract
        )

        emb = psum_mx.tile([P, DIM], F32)
        for g in range(PASSES):
            nc.tensor.matmul_mx(
                out=emb[:],
                lhsT=x_codes[:, g, :].bitcast(FP8X4),
                lhsT_scale=x_scales[:, g, :],
                rhs=w_codes[g][:].bitcast(FP8X4),
                rhs_scale=w_scales[g][:],
                start=(g == 0),
                stop=(g == PASSES - 1),
            )
        pe_squares = keep.tile([P, PE_PIXELS], F32)
        nc.scalar.activation(
            out=pe_squares[:], in_=pe_diff[:, 0:PE_PIXELS], func=ACT.Square, accum_out=diff_norm[:, 0:1]
        )
        first, last = diff[:, 0:SCALAR_PIXELS], diff[:, SCALAR_PIXELS:]
        nc.scalar.activation(out=first, in_=first, func=ACT.Square, accum_out=diff_norm[:, 1:2])

        emb_squares = keep.tile([P, DIM], F32)
        emb_norm = keep.tile([P, 1], F32)
        nc.scalar.activation(out=emb_squares[:], in_=emb[:], func=ACT.Square, accum_out=emb_norm[:])
        ceiling = keep.tile([P, 1], F32)
        nc.scalar.activation(
            out=ceiling[:], in_=emb_norm[:], func=ACT.Copy, scale=0.5, bias=-0.5 * MARGIN * MARGIN
        )

        dots = []
        for block in range(CHAINS):
            dots.append(psum_mx.tile([P, BATCH], F32, name="dots%d" % block)[:])
        for pair in range((BLOCKS - CHAINS) // 2):
            bank = psum_plain.tile([P, BANK], F32, tag="plain", name="dots")
            dots.extend([bank[:, 0:BATCH], bank[:, BATCH : 2 * BATCH]])
        for block in range(BLOCKS):
            nc.tensor.matmul_mx(
                out=dots[block],
                lhsT=lk_codes[block // PER_PIECE][:, block % PER_PIECE, :].bitcast(FP8X4),
                lhsT_scale=lk_scales[block // PER_PIECE][:, block % PER_PIECE, :],
                rhs=emb_codes[:].bitcast(FP8X4),
                rhs_scale=emb_scales[:],
                start=True,
                stop=True,
            )
        best = keep.tile([P, CHAINS, BATCH], F32)
        for block in range(BLOCKS):
            running = best[:, block % CHAINS, :]
            scores = dots[block]
            half_norm = lk_half_norm_1[:] if block == 1 else lk_half_norm[:, block : block + 1]
            if block < CHAINS:
                nc.vector.tensor_scalar(
                    out=running, in0=scores, scalar1=half_norm, scalar2=None, op0=ALU.subtract
                )
            else:
                nc.vector.scalar_tensor_tensor(
                    out=running, in0=scores, scalar=half_norm, in1=running,
                    op0=ALU.subtract, op1=ALU.max,
                )

        nc.vector.scalar_tensor_tensor(
            out=last, in0=last, scalar=1.0, in1=last, op0=ALU.mult, op1=ALU.mult, accum_out=diff_norm[:, 2:3]
        )

        best_t = psum_plain.tile([P, BANK], F32, tag="plain")
        for chain in range(CHAINS):
            nc.tensor.transpose(best_t[:, P * chain : P * (chain + 1)], best[:, chain, :], ident[:])
        capped = keep.tile([P, P * CHAINS], F32)
        top = keep.tile([P, 1], F32)
        nc.vector.tensor_scalar(
            out=capped[:], in0=best_t[:, 0 : P * CHAINS], scalar1=ceiling[:], scalar2=None,
            op0=ALU.min, op1=ALU.max, accum_out=top[:],
        )
        dist = keep.tile([P, 1], F32)
        nc.scalar.activation(out=dist[:], in_=top[:], func=ACT.Sqrt, scale=-2.0, bias=emb_norm[:])

        sums = psum_plain.tile([P, 4], F32, tag="plain", name="sums")
        nc.tensor.matmul(out=sums[:], lhsT=mean_weight[:], rhs=diff_norm[:], start=True, stop=True)
        base = keep.tile([P, 1], F32)
        nc.vector.tensor_reduce(out=base[:], in_=sums[:], axis=mybir.AxisListType.X, op=ALU.add)

        nc.vector.tensor_scalar(
            out=column[:, 0:1], in0=dist[:], scalar1=-SCALE, scalar2=base[:],
            op0=ALU.mult, op1=ALU.add,
        )
        rows = keep.tile([P, SQUARE], F32, align_bytes=64)
        nc.vector.transpose(out=rows[:], in_=column[:])
        nc.sync.dma_start(out=out.rearrange("(q b) -> q b", b=SQUARE), in_=rows[0:P:SQUARE, :])
